import numpy as np
import ml_dtypes


def mxq(x, axis, fmt="e4m3"):
    dtype, down = {"e4m3": (ml_dtypes.float8_e4m3fn, 7), "e5m2": (ml_dtypes.float8_e5m2, 14)}[fmt]
    v = np.moveaxis(np.asarray(x, np.float32).astype(ml_dtypes.bfloat16).astype(np.float64), axis, -1)
    blocks = v.reshape(v.shape[:-1] + (-1, 32))
    amax = np.abs(blocks).max(-1, keepdims=True)
    byte = np.maximum(np.where(amax > 0, np.frexp(amax)[1] - 1 + 127, 0) - down, 1)
    scale = np.exp2(byte - 127.0)
    codes = (blocks / scale).astype(np.float32).astype(dtype).astype(np.float64)
    return np.moveaxis((codes * scale).reshape(v.shape), -1, axis)


WIDE = False


def mx_kscale(k):
    if not WIDE:
        return np.ones(k)
    levels = np.array([10, -10, 5, -5, 0])
    a = np.random.permutation(np.resize(levels, k // 512 * 4)).reshape(k // 512, 4)
    idx = np.arange(k)
    return np.exp2(a[idx // 512, idx % 128 // 32])


BF16 = ml_dtypes.bfloat16


def bf(x):
    return np.asarray(x, np.float32).astype(BF16)


def f64(x):
    return np.asarray(x).astype(np.float64)


B, C, P, NH, G, HH, WW = 4, 2048, 512, 32, 16, 16, 32
N = HH * WW
EPS = 1e-5


def group_norm(x, gamma, beta):
    xg = x.reshape(B, G, (C // G) * N)
    mean = xg.mean(axis=-1, keepdims=True)
    var = xg.var(axis=-1, keepdims=True)
    xn = ((xg - mean) / np.sqrt(var + EPS)).reshape(B, C, N)
    return xn * gamma[None, :, None] + beta[None, :, None]


def setup_inputs():
    s = mx_kscale(P)
    return {
        "feat": bf(np.random.standard_normal((B, C, HH, WW))),
        "h_attn": bf(np.random.standard_normal((B, P, HH, WW)) * 0.5 * s[None, :, None, None]),
        "w_out": bf(np.random.standard_normal((C, P)) * 2.0 / np.sqrt(P) / s[None, :]),
        "b_out": bf(np.random.standard_normal(C) * 0.3),
        "gamma": bf(1.0 + 0.1 * np.random.standard_normal(C)),
        "beta": bf(0.1 * np.random.standard_normal(C)),
    }


def reference(feat, h_attn, w_out, b_out, gamma, beta):
    y = (mxq(f64(w_out), 1, "e4m3") @ mxq(f64(h_attn).reshape(B, P, N), 1, "e4m3")) + f64(b_out)[None, :, None]
    x = f64(feat).reshape(B, C, N) + y
    return group_norm(x, f64(gamma), f64(beta)).reshape(B, C, HH, WW)

@@ -1,0 +1,229 @@
+from contextlib import ExitStack
+
+import concourse.mybir as mybir
+from concourse.masks import make_identity
+
+F32 = mybir.dt.float32
+BF16 = mybir.dt.bfloat16
+U32 = mybir.dt.uint32
+U8 = mybir.dt.uint8
+FP8X4 = mybir.dt.float8_e4m3fn_x4
+ALU = mybir.AluOpType
+ACT = mybir.ActivationFunctionType
+AX = mybir.AxisListType
+
+P = 128
+PACK = 4
+BATCH = 4
+CHANNELS = 2048
+K = 512
+N = 512
+GROUP = 128
+EPS = 1e-5
+
+ROWS = 4
+SLAB = P * ROWS
+SLABS = CHANNELS // SLAB
+QUADRANT = GROUP // ROWS
+
+FLOPS = 2 * BATCH * CHANNELS * K * N
+
+
+def tile_crossattention_pa_kernel(tc, feat, h_attn, w_out, b_out, gamma, beta, out):
+    nc = tc.nc
+
+    feat_v = feat.rearrange("b (s p j) h w -> b s p j (h w)", p=P, j=ROWS)
+    out_v = out.rearrange("b (s p j) h w -> b s p j (h w)", p=P, j=ROWS)
+    w_v = w_out.rearrange("(s p j) k -> s p j k", p=P, j=ROWS)
+    h_v = h_attn.rearrange("b (u q e) h w -> b q u e (h w)", u=2, e=2)
+
+    with ExitStack() as ctx:
+        const = ctx.enter_context(tc.tile_pool(name="const", bufs=1))
+        raw = ctx.enter_context(tc.tile_pool(name="raw", bufs=4))
+        grouped = ctx.enter_context(tc.tile_pool(name="grouped", bufs=2))
+        feats = ctx.enter_context(tc.tile_pool(name="feats", bufs=BATCH * SLABS))
+        xs = ctx.enter_context(tc.tile_pool(name="xs", bufs=6))
+        junk = ctx.enter_context(tc.tile_pool(name="junk", bufs=2))
+        small = ctx.enter_context(tc.tile_pool(name="small", bufs=4))
+        psum_y = ctx.enter_context(tc.psum_pool(name="psum_y", bufs=5))
+        psum_t = ctx.enter_context(tc.psum_pool(name="psum_t", bufs=2))
+        psum_s = ctx.enter_context(tc.psum_pool(name="psum_s", bufs=1))
+
+        h_raw = {}
+        w_raw = {}
+        feat_sb = {}
+
+        def load_h(b):
+            h_tile = raw.tile([P, PACK, N], BF16)
+            nc.sync.dma_start(out=h_tile[:].rearrange("q (u e) n -> q u e n", u=2), in_=h_v[b])
+            h_raw[b] = h_tile
+
+        def load_w(s):
+            w_tile = raw.tile([P, ROWS, K], BF16)
+            nc.sync.dma_start(out=w_tile[:], in_=w_v[s])
+            w_raw[s] = w_tile
+
+        def load_feat(b, s):
+            feat_tile = feats.tile([P, ROWS, N], BF16)
+            nc.sync.dma_start(out=feat_tile[:], in_=feat_v[b, s])
+            feat_sb[(b, s)] = feat_tile
+
+        params_bf = const.tile([P, 3, SLABS, ROWS], BF16)
+        for which, vec in enumerate((b_out, gamma, beta)):
+            nc.scalar.dma_start(
+                out=params_bf[:, which], in_=vec.rearrange("(s p j) -> p s j", p=P, j=ROWS)
+            )
+
+        load_h(0)
+        for s in range(SLABS):
+            load_w(s)
+            load_feat(0, s)
+        for b in range(1, BATCH):
+            load_h(b)
+            for s in range(SLABS):
+                load_feat(b, s)
+
+        eps = const.tile([P, 1], F32)
+        nc.vector.memset(eps[:], EPS)
+        warm = const.tile([P, 1], F32)
+        nc.scalar.activation(out=warm[:], in_=eps[:], func=ACT.Abs_reciprocal_sqrt)
+
+        ident = const.tile([P, P], F32)
+        make_identity(nc, ident[:])
+
+        group_avg = const.tile([P, P], F32)
+        nc.vector.memset(group_avg[:], 0.0)
+        for g in range(P // QUADRANT):
+            rows = slice(g * QUADRANT, (g + 1) * QUADRANT)
+            nc.vector.memset(group_avg[rows, rows], -1.0 / (GROUP * N))
+
+        params = const.tile([P, 3, SLABS, ROWS], F32)
+        nc.vector.tensor_copy(out=params[:], in_=params_bf[:])
+
+        w_codes = const.tile([P, SLABS, SLAB], U32, align_bytes=64)
+        w_scales = const.tile([P, SLABS, SLAB], U8, align_bytes=64)
+        h_codes = const.tile([P, BATCH, N], U32, align_bytes=64)
+        h_scales = const.tile([P, BATCH, N], U8, align_bytes=64)
+
+        def quantise_h(b):
+            h_grouped = grouped.tile([P, N, PACK], BF16, align_bytes=64)
+            nc.vector.tensor_copy(
+                out=h_grouped[:].rearrange("q (c i) t -> q c t i", i=4),
+                in_=h_raw[b][:].rearrange("q t (c i) -> q c t i", i=4),
+            )
+            nc.vector.quantize_mx(
+                out=h_codes[:, b, :].bitcast(FP8X4),
+                scales=h_scales[:, b, :],
+                in_=h_grouped[:].rearrange("q n t -> q (n t)"),
+            )
+
+        def quantise_w(s):
+            w_words = w_raw[s][:].rearrange("p j k -> p (j k)").bitcast(F32)
+            w_grouped = grouped.tile([P, ROWS * P * PACK], BF16, align_bytes=64)
+            w_grouped_words = w_grouped[:].bitcast(F32).rearrange(
+                "q (j p u) -> q j p u", j=ROWS, u=2
+            )
+            for half in range(2):
+                w_t = psum_t.tile([P, 2, 2, P], F32)
+                for jj in range(2):
+                    for u in range(2):
+                        first = ((2 * half + jj) * 2 + u) * P
+                        nc.tensor.transpose(w_t[:, jj, u, :], w_words[:, first : first + P], ident[:])
+                nc.scalar.copy(
+                    out=w_grouped_words[:, 2 * half : 2 * half + 2],
+                    in_=w_t[:].rearrange("q jj u p -> q jj p u"),
+                )
+            nc.vector.quantize_mx(
+                out=w_codes[:, s, :].bitcast(FP8X4),
+                scales=w_scales[:, s, :],
+                in_=w_grouped[:],
+            )
+
+        for b in range(BATCH):
+            quantise_h(b)
+            for s in range(SLABS):
+                if b == 0:
+                    quantise_w(s)
+
+                x = xs.tile([P, ROWS, N], F32)
+                sums = small.tile([P, ROWS + 1, 8], F32)
+                for j in range(ROWS):
+                    y = psum_y.tile([P, N], F32)
+                    cols = slice(j * P, (j + 1) * P)
+                    nc.tensor.matmul_mx(
+                        out=y[:],
+                        lhsT=w_codes[:, s, cols].bitcast(FP8X4),
+                        lhsT_scale=w_scales[:, s, cols],
+                        rhs=h_codes[:, b, :].bitcast(FP8X4),
+                        rhs_scale=h_scales[:, b, :],
+                        start=True,
+                        stop=True,
+                    )
+                    nc.vector.scalar_tensor_tensor(
+                        out=x[:, j, :],
+                        in0=y[:],
+                        scalar=params[:, 0, s, j : j + 1],
+                        in1=feat_sb[(b, s)][:, j, :],
+                        op0=ALU.add,
+                        op1=ALU.add,
+                        accum_out=sums[:, j, 0:1],
+                    )
+                squares = junk.tile([P, ROWS * N], BF16)
+                nc.scalar.activation(
+                    out=squares[:],
+                    in_=x[:].rearrange("p j n -> p (j n)"),
+                    func=ACT.Square,
+                    accum_out=sums[:, ROWS, 0:1],
+                )
+
+                moments = psum_s.tile([P, ROWS + 1], F32)
+                nc.tensor.matmul(
+                    out=moments[:], lhsT=group_avg[:], rhs=sums[:, :, 0], start=True, stop=True
+                )
+                neg_mean = small.tile([P, 1], F32)
+                nc.vector.tensor_reduce(out=neg_mean[:], in_=moments[:, 0:ROWS], axis=AX.X, op=ALU.add)
+                neg_var = small.tile([P, 1], F32)
+                nc.vector.scalar_tensor_tensor(
+                    out=neg_var[:],
+                    in0=neg_mean[:],
+                    scalar=neg_mean[:, 0:1],
+                    in1=moments[:, ROWS : ROWS + 1],
+                    op0=ALU.mult,
+                    op1=ALU.add,
+                )
+                rstd = small.tile([P, 1], F32)
+                nc.scalar.activation(
+                    out=rstd[:], in_=neg_var[:], func=ACT.Abs_reciprocal_sqrt, bias=eps[:, 0:1], scale=-1.0
+                )
+                gain = small.tile([P, ROWS], F32)
+                nc.vector.tensor_scalar(
+                    out=gain[:], in0=params[:, 1, s, :], scalar1=rstd[:, 0:1], scalar2=None, op0=ALU.mult
+                )
+                shift = small.tile([P, ROWS], F32)
+                nc.vector.scalar_tensor_tensor(
+                    out=shift[:],
+                    in0=gain[:],
+                    scalar=neg_mean[:, 0:1],
+                    in1=params[:, 2, s, :],
+                    op0=ALU.mult,
+                    op1=ALU.add,
+                )
+                for j in range(ROWS):
+                    if j < 2:
+                        nc.vector.tensor_scalar(
+                            out=x[:, j, :],
+                            in0=x[:, j, :],
+                            scalar1=gain[:, j : j + 1],
+                            scalar2=shift[:, j : j + 1],
+                            op0=ALU.mult,
+                            op1=ALU.add,
+                        )
+                    else:
+                        nc.scalar.activation(
+                            out=x[:, j, :],
+                            in_=x[:, j, :],
+                            func=ACT.Identity,
+                            bias=shift[:, j : j + 1],
+                            scale=gain[:, j : j + 1],
+                        )
+                nc.sync.dma_start(out=out_v[b, s], in_=x[:])

@@ -24,16 +24,21 @@ EPS = 1e-5
 ROWS = 4
 SLAB = P * ROWS
 SLABS = CHANNELS // SLAB
+TOTAL = BATCH * SLABS
 QUADRANT = GROUP // ROWS
 
 FLOPS = 2 * BATCH * CHANNELS * K * N
+
+HALF = ROWS // 2
+ROWS_ON_SCALAR = 1
+AHEAD = 16
 
 
 def tile_crossattention_pa_kernel(tc, feat, h_attn, w_out, b_out, gamma, beta, out):
     nc = tc.nc
 
-    feat_v = feat.rearrange("b (s p j) h w -> b s p j (h w)", p=P, j=ROWS)
-    out_v = out.rearrange("b (s p j) h w -> b s p j (h w)", p=P, j=ROWS)
+    feat_v = feat.rearrange("b (s p j) h w -> (b s) p j (h w)", p=P, j=ROWS)
+    out_v = out.rearrange("b (s p j) h w -> (b s) p j (h w)", p=P, j=ROWS)
     w_v = w_out.rearrange("(s p j) k -> s p j k", p=P, j=ROWS)
     h_v = h_attn.rearrange("b (u q e) h w -> b q u e (h w)", u=2, e=2)
 
@@ -41,47 +46,13 @@ def tile_crossattention_pa_kernel(tc, feat, h_attn, w_out, b_out, gamma, beta, o
         const = ctx.enter_context(tc.tile_pool(name="const", bufs=1))
         raw = ctx.enter_context(tc.tile_pool(name="raw", bufs=4))
         grouped = ctx.enter_context(tc.tile_pool(name="grouped", bufs=2))
-        feats = ctx.enter_context(tc.tile_pool(name="feats", bufs=BATCH * SLABS))
-        xs = ctx.enter_context(tc.tile_pool(name="xs", bufs=6))
-        junk = ctx.enter_context(tc.tile_pool(name="junk", bufs=2))
+        feats = ctx.enter_context(tc.tile_pool(name="feats", bufs=16))
+        xs = ctx.enter_context(tc.tile_pool(name="xs", bufs=8))
+        junk = ctx.enter_context(tc.tile_pool(name="junk", bufs=3))
         small = ctx.enter_context(tc.tile_pool(name="small", bufs=4))
         psum_y = ctx.enter_context(tc.psum_pool(name="psum_y", bufs=5))
         psum_t = ctx.enter_context(tc.psum_pool(name="psum_t", bufs=2))
         psum_s = ctx.enter_context(tc.psum_pool(name="psum_s", bufs=1))
-
-        h_raw = {}
-        w_raw = {}
-        feat_sb = {}
-
-        def load_h(b):
-            h_tile = raw.tile([P, PACK, N], BF16)
-            nc.sync.dma_start(out=h_tile[:].rearrange("q (u e) n -> q u e n", u=2), in_=h_v[b])
-            h_raw[b] = h_tile
-
-        def load_w(s):
-            w_tile = raw.tile([P, ROWS, K], BF16)
-            nc.sync.dma_start(out=w_tile[:], in_=w_v[s])
-            w_raw[s] = w_tile
-
-        def load_feat(b, s):
-            feat_tile = feats.tile([P, ROWS, N], BF16)
-            nc.sync.dma_start(out=feat_tile[:], in_=feat_v[b, s])
-            feat_sb[(b, s)] = feat_tile
-
-        params_bf = const.tile([P, 3, SLABS, ROWS], BF16)
-        for which, vec in enumerate((b_out, gamma, beta)):
-            nc.scalar.dma_start(
-                out=params_bf[:, which], in_=vec.rearrange("(s p j) -> p s j", p=P, j=ROWS)
-            )
-
-        load_h(0)
-        for s in range(SLABS):
-            load_w(s)
-            load_feat(0, s)
-        for b in range(1, BATCH):
-            load_h(b)
-            for s in range(SLABS):
-                load_feat(b, s)
 
         eps = const.tile([P, 1], F32)
         nc.vector.memset(eps[:], EPS)
@@ -97,133 +68,239 @@ def tile_crossattention_pa_kernel(tc, feat, h_attn, w_out, b_out, gamma, beta, o
             rows = slice(g * QUADRANT, (g + 1) * QUADRANT)
             nc.vector.memset(group_avg[rows, rows], -1.0 / (GROUP * N))
 
+        params_bf = const.tile([P, 3, SLABS, ROWS], BF16)
+        for which, vec in enumerate((b_out, gamma, beta)):
+            nc.scalar.dma_start(
+                out=params_bf[:, which], in_=vec.rearrange("(s p j) -> p s j", p=P, j=ROWS)
+            )
         params = const.tile([P, 3, SLABS, ROWS], F32)
-        nc.vector.tensor_copy(out=params[:], in_=params_bf[:])
 
         w_codes = const.tile([P, SLABS, SLAB], U32, align_bytes=64)
         w_scales = const.tile([P, SLABS, SLAB], U8, align_bytes=64)
         h_codes = const.tile([P, BATCH, N], U32, align_bytes=64)
         h_scales = const.tile([P, BATCH, N], U8, align_bytes=64)
 
-        def quantise_h(b):
-            h_grouped = grouped.tile([P, N, PACK], BF16, align_bytes=64)
-            nc.vector.tensor_copy(
-                out=h_grouped[:].rearrange("q (c i) t -> q c t i", i=4),
-                in_=h_raw[b][:].rearrange("q t (c i) -> q c t i", i=4),
-            )
-            nc.vector.quantize_mx(
-                out=h_codes[:, b, :].bitcast(FP8X4),
-                scales=h_scales[:, b, :],
-                in_=h_grouped[:].rearrange("q n t -> q (n t)"),
-            )
+        h_raw = {}
+        w_raw = {}
+        h_grouped = {}
+        w_grouped = {}
+        feat_sb = {}
+        y_ps = {}
+        x_sb = {}
+        sums_sb = {}
+        mom_ps = {}
+        neg_mean_sb = {}
+        neg_var_sb = {}
+        rstd_sb = {}
+        gain_sb = {}
+        shift_sb = {}
 
-        def quantise_w(s):
-            w_words = w_raw[s][:].rearrange("p j k -> p (j k)").bitcast(F32)
-            w_grouped = grouped.tile([P, ROWS * P * PACK], BF16, align_bytes=64)
-            w_grouped_words = w_grouped[:].bitcast(F32).rearrange(
-                "q (j p u) -> q j p u", j=ROWS, u=2
-            )
-            for half in range(2):
-                w_t = psum_t.tile([P, 2, 2, P], F32)
-                for jj in range(2):
-                    for u in range(2):
-                        first = ((2 * half + jj) * 2 + u) * P
-                        nc.tensor.transpose(w_t[:, jj, u, :], w_words[:, first : first + P], ident[:])
-                nc.scalar.copy(
-                    out=w_grouped_words[:, 2 * half : 2 * half + 2],
-                    in_=w_t[:].rearrange("q jj u p -> q jj p u"),
+        def load_operands(i):
+            b, s = divmod(i, SLABS)
+            if i < TOTAL and b == 0:
+                w_tile = raw.tile([P, ROWS, K], BF16)
+                nc.sync.dma_start(out=w_tile[:], in_=w_v[s])
+                w_raw[s] = w_tile
+            if i < TOTAL and s == 0:
+                h_tile = raw.tile([P, PACK, N], BF16)
+                nc.sync.dma_start(out=h_tile[:].rearrange("q (u e) n -> q u e n", u=2), in_=h_v[b])
+                h_raw[b] = h_tile
+
+        def load_feat(i):
+            if i < TOTAL:
+                feat_tile = feats.tile([P, ROWS, N], BF16)
+                nc.sync.dma_start(out=feat_tile[:], in_=feat_v[i])
+                feat_sb[i] = feat_tile
+
+        def regroup(i):
+            b, s = divmod(i, SLABS)
+            if b == 0:
+                w_words = w_raw[s][:].rearrange("p j k -> p (j k)").bitcast(F32)
+                w_group = grouped.tile([P, ROWS * P * PACK], BF16, align_bytes=64)
+                w_group_words = w_group[:].bitcast(F32).rearrange("q (j p u) -> q j p u", j=ROWS, u=2)
+                for half in range(2):
+                    w_t = psum_t.tile([P, 2, 2, P], F32)
+                    for jj in range(2):
+                        for u in range(2):
+                            first = ((2 * half + jj) * 2 + u) * P
+                            nc.tensor.transpose(w_t[:, jj, u, :], w_words[:, first : first + P], ident[:])
+                    nc.scalar.copy(
+                        out=w_group_words[:, 2 * half : 2 * half + 2],
+                        in_=w_t[:].rearrange("q jj u p -> q jj p u"),
+                    )
+                w_grouped[s] = w_group
+            if s == 0:
+                h_group = grouped.tile([P, N, PACK], BF16, align_bytes=64)
+                nc.vector.tensor_copy(
+                    out=h_group[:].rearrange("q (c i) t -> q c t i", i=4),
+                    in_=h_raw[b][:].rearrange("q t (c i) -> q c t i", i=4),
                 )
-            nc.vector.quantize_mx(
-                out=w_codes[:, s, :].bitcast(FP8X4),
-                scales=w_scales[:, s, :],
-                in_=w_grouped[:],
-            )
+                h_grouped[b] = h_group
 
-        for b in range(BATCH):
-            quantise_h(b)
-            for s in range(SLABS):
-                if b == 0:
-                    quantise_w(s)
+        def quantise(i):
+            b, s = divmod(i, SLABS)
+            if b == 0:
+                nc.vector.quantize_mx(
+                    out=w_codes[:, s, :].bitcast(FP8X4), scales=w_scales[:, s, :], in_=w_grouped[s][:]
+                )
+            if s == 0:
+                nc.vector.quantize_mx(
+                    out=h_codes[:, b, :].bitcast(FP8X4),
+                    scales=h_scales[:, b, :],
+                    in_=h_grouped[b][:].rearrange("q n t -> q (n t)"),
+                )
 
+        def project(i, half):
+            b, s = divmod(i, SLABS)
+            for j in range(half * HALF, (half + 1) * HALF):
+                y = psum_y.tile([P, N], F32)
+                cols = slice(j * P, (j + 1) * P)
+                nc.tensor.matmul_mx(
+                    out=y[:],
+                    lhsT=w_codes[:, s, cols].bitcast(FP8X4),
+                    lhsT_scale=w_scales[:, s, cols],
+                    rhs=h_codes[:, b, :].bitcast(FP8X4),
+                    rhs_scale=h_scales[:, b, :],
+                    start=True,
+                    stop=True,
+                )
+                y_ps[(i, j)] = y
+
+        def residual(i, half):
+            s = i % SLABS
+            if half == 0:
                 x = xs.tile([P, ROWS, N], F32)
-                sums = small.tile([P, ROWS + 1, 8], F32)
-                for j in range(ROWS):
-                    y = psum_y.tile([P, N], F32)
-                    cols = slice(j * P, (j + 1) * P)
-                    nc.tensor.matmul_mx(
-                        out=y[:],
-                        lhsT=w_codes[:, s, cols].bitcast(FP8X4),
-                        lhsT_scale=w_scales[:, s, cols],
-                        rhs=h_codes[:, b, :].bitcast(FP8X4),
-                        rhs_scale=h_scales[:, b, :],
-                        start=True,
-                        stop=True,
-                    )
-                    nc.vector.scalar_tensor_tensor(
-                        out=x[:, j, :],
-                        in0=y[:],
-                        scalar=params[:, 0, s, j : j + 1],
-                        in1=feat_sb[(b, s)][:, j, :],
-                        op0=ALU.add,
-                        op1=ALU.add,
-                        accum_out=sums[:, j, 0:1],
-                    )
-                squares = junk.tile([P, ROWS * N], BF16)
-                nc.scalar.activation(
-                    out=squares[:],
-                    in_=x[:].rearrange("p j n -> p (j n)"),
-                    func=ACT.Square,
-                    accum_out=sums[:, ROWS, 0:1],
+                x_sb[i] = x
+                sums = small.tile([P, 2, HALF + 1, 8], F32)
+                sums_sb[i] = sums
+            for r in range(HALF):
+                j = half * HALF + r
+                nc.vector.scalar_tensor_tensor(
+                    out=x_sb[i][:, j, :],
+                    in0=y_ps[(i, j)][:],
+                    scalar=params[:, 0, s, j : j + 1],
+                    in1=feat_sb[i][:, j, :],
+                    op0=ALU.add,
+                    op1=ALU.add,
+                    accum_out=sums_sb[i][:, half, r, 0:1],
                 )
 
-                moments = psum_s.tile([P, ROWS + 1], F32)
-                nc.tensor.matmul(
-                    out=moments[:], lhsT=group_avg[:], rhs=sums[:, :, 0], start=True, stop=True
-                )
-                neg_mean = small.tile([P, 1], F32)
-                nc.vector.tensor_reduce(out=neg_mean[:], in_=moments[:, 0:ROWS], axis=AX.X, op=ALU.add)
-                neg_var = small.tile([P, 1], F32)
-                nc.vector.scalar_tensor_tensor(
-                    out=neg_var[:],
-                    in0=neg_mean[:],
-                    scalar=neg_mean[:, 0:1],
-                    in1=moments[:, ROWS : ROWS + 1],
-                    op0=ALU.mult,
-                    op1=ALU.add,
-                )
-                rstd = small.tile([P, 1], F32)
-                nc.scalar.activation(
-                    out=rstd[:], in_=neg_var[:], func=ACT.Abs_reciprocal_sqrt, bias=eps[:, 0:1], scale=-1.0
-                )
-                gain = small.tile([P, ROWS], F32)
-                nc.vector.tensor_scalar(
-                    out=gain[:], in0=params[:, 1, s, :], scalar1=rstd[:, 0:1], scalar2=None, op0=ALU.mult
-                )
-                shift = small.tile([P, ROWS], F32)
-                nc.vector.scalar_tensor_tensor(
-                    out=shift[:],
-                    in0=gain[:],
-                    scalar=neg_mean[:, 0:1],
-                    in1=params[:, 2, s, :],
-                    op0=ALU.mult,
-                    op1=ALU.add,
-                )
-                for j in range(ROWS):
-                    if j < 2:
-                        nc.vector.tensor_scalar(
-                            out=x[:, j, :],
-                            in0=x[:, j, :],
-                            scalar1=gain[:, j : j + 1],
-                            scalar2=shift[:, j : j + 1],
-                            op0=ALU.mult,
-                            op1=ALU.add,
-                        )
-                    else:
-                        nc.scalar.activation(
-                            out=x[:, j, :],
-                            in_=x[:, j, :],
-                            func=ACT.Identity,
-                            bias=shift[:, j : j + 1],
-                            scale=gain[:, j : j + 1],
-                        )
-                nc.sync.dma_start(out=out_v[b, s], in_=x[:])
+        def squares(i, half):
+            sq = junk.tile([P, HALF * N], BF16)
+            nc.scalar.activation(
+                out=sq[:],
+                in_=x_sb[i][:, half * HALF : (half + 1) * HALF, :].rearrange("p j n -> p (j n)"),
+                func=ACT.Square,
+                accum_out=sums_sb[i][:, half, HALF, 0:1],
+            )
+            if half == 0:
+                mom = psum_s.tile([P, HALF + 1], F32)
+                mom_ps[i] = mom
+            nc.tensor.matmul(
+                out=mom_ps[i][:],
+                lhsT=group_avg[:],
+                rhs=sums_sb[i][:, half, :, 0],
+                start=(half == 0),
+                stop=(half == 1),
+            )
+
+        def moments(i):
+            mom = mom_ps[i]
+            neg_mean = small.tile([P, 1], F32)
+            nc.vector.tensor_reduce(out=neg_mean[:], in_=mom[:, 0:HALF], axis=AX.X, op=ALU.add)
+            neg_var = small.tile([P, 1], F32)
+            nc.vector.scalar_tensor_tensor(
+                out=neg_var[:],
+                in0=neg_mean[:],
+                scalar=neg_mean[:, 0:1],
+                in1=mom[:, HALF : HALF + 1],
+                op0=ALU.mult,
+                op1=ALU.add,
+            )
+            neg_mean_sb[i] = neg_mean
+            neg_var_sb[i] = neg_var
+
+        def inv_std(i):
+            rstd = small.tile([P, 1], F32)
+            nc.scalar.activation(
+                out=rstd[:], in_=neg_var_sb[i][:], func=ACT.Abs_reciprocal_sqrt, bias=eps[:, 0:1], scale=-1.0
+            )
+            rstd_sb[i] = rstd
+
+        def affine(i):
+            s = i % SLABS
+            gain = small.tile([P, ROWS], F32)
+            nc.vector.tensor_scalar(
+                out=gain[:], in0=params[:, 1, s, :], scalar1=rstd_sb[i][:, 0:1], scalar2=None, op0=ALU.mult
+            )
+            shift = small.tile([P, ROWS], F32)
+            nc.vector.scalar_tensor_tensor(
+                out=shift[:],
+                in0=gain[:],
+                scalar=neg_mean_sb[i][:, 0:1],
+                in1=params[:, 2, s, :],
+                op0=ALU.mult,
+                op1=ALU.add,
+            )
+            gain_sb[i] = gain
+            shift_sb[i] = shift
+
+        def normalise(i):
+            x = x_sb[i]
+            helper = nc.vector if i == TOTAL - 1 else nc.gpsimd
+            for j in range(ROWS):
+                gain_j = gain_sb[i][:, j : j + 1]
+                shift_j = shift_sb[i][:, j : j + 1]
+                if j < ROWS_ON_SCALAR:
+                    nc.scalar.activation(out=x[:, j, :], in_=x[:, j, :], func=ACT.Identity, bias=shift_j, scale=gain_j)
+                else:
+                    helper.tensor_scalar(
+                        out=x[:, j, :], in0=x[:, j, :], scalar1=gain_j, scalar2=shift_j, op0=ALU.mult, op1=ALU.add
+                    )
+            for half in range(2):
+                rows = slice(half * HALF, (half + 1) * HALF)
+                nc.sync.dma_start(out=out_v[i][:, rows, :], in_=x[:, rows, :])
+
+
+        load_operands(0)
+        load_operands(1)
+        for i in range(AHEAD):
+            load_feat(i)
+            load_operands(i + 2)
+
+        regroup(0)
+        regroup(1)
+        quantise(0)
+        nc.vector.tensor_copy(out=params[:], in_=params_bf[:])
+        project(0, 0)
+        project(0, 1)
+
+        for step in range(TOTAL + 1):
+            here = step < TOTAL
+            before = step >= 1
+            after = step + 1 < TOTAL
+            load_feat(step + AHEAD)
+            load_operands(step + AHEAD + 2)
+            if step + 2 < TOTAL:
+                regroup(step + 2)
+            if here:
+                residual(step, 0)
+            if before:
+                moments(step - 1)
+            if after:
+                quantise(step + 1)
+                project(step + 1, 0)
+            if here:
+                squares(step, 0)
+            if before:
+                inv_std(step - 1)
+            if here:
+                residual(step, 1)
+            if after:
+                project(step + 1, 1)
+            if before:
+                affine(step - 1)
+            if here:
+                squares(step, 1)
+            if before:
+                normalise(step - 1)

@@ -30,8 +30,7 @@ QUADRANT = GROUP // ROWS
 FLOPS = 2 * BATCH * CHANNELS * K * N
 
 HALF = ROWS // 2
-ROWS_ON_SCALAR = 1
-AHEAD = 16
+ROWS_ON_VECTOR = 1
 
 
 def tile_crossattention_pa_kernel(tc, feat, h_attn, w_out, b_out, gamma, beta, out):
@@ -46,13 +45,12 @@ def tile_crossattention_pa_kernel(tc, feat, h_attn, w_out, b_out, gamma, beta, o
         const = ctx.enter_context(tc.tile_pool(name="const", bufs=1))
         raw = ctx.enter_context(tc.tile_pool(name="raw", bufs=4))
         grouped = ctx.enter_context(tc.tile_pool(name="grouped", bufs=2))
-        feats = ctx.enter_context(tc.tile_pool(name="feats", bufs=16))
+        feats = ctx.enter_context(tc.tile_pool(name="feats", bufs=TOTAL))
         xs = ctx.enter_context(tc.tile_pool(name="xs", bufs=8))
-        junk = ctx.enter_context(tc.tile_pool(name="junk", bufs=3))
+        junk = ctx.enter_context(tc.tile_pool(name="junk", bufs=2))
         small = ctx.enter_context(tc.tile_pool(name="small", bufs=4))
-        psum_y = ctx.enter_context(tc.psum_pool(name="psum_y", bufs=5))
-        psum_t = ctx.enter_context(tc.psum_pool(name="psum_t", bufs=2))
-        psum_s = ctx.enter_context(tc.psum_pool(name="psum_s", bufs=1))
+        psum_y = ctx.enter_context(tc.psum_pool(name="psum_y", bufs=4))
+        psum_aux = ctx.enter_context(tc.psum_pool(name="psum_aux", bufs=4))
 
         eps = const.tile([P, 1], F32)
         nc.vector.memset(eps[:], EPS)
@@ -82,44 +80,32 @@ def tile_crossattention_pa_kernel(tc, feat, h_attn, w_out, b_out, gamma, beta, o
 
         h_raw = {}
         w_raw = {}
-        h_grouped = {}
-        w_grouped = {}
         feat_sb = {}
-        y_ps = {}
-        x_sb = {}
-        sums_sb = {}
-        mom_ps = {}
-        neg_mean_sb = {}
-        neg_var_sb = {}
-        rstd_sb = {}
-        gain_sb = {}
-        shift_sb = {}
 
         def load_operands(i):
             b, s = divmod(i, SLABS)
-            if i < TOTAL and b == 0:
+            if b == 0:
                 w_tile = raw.tile([P, ROWS, K], BF16)
                 nc.sync.dma_start(out=w_tile[:], in_=w_v[s])
                 w_raw[s] = w_tile
-            if i < TOTAL and s == 0:
+            if s == 0:
                 h_tile = raw.tile([P, PACK, N], BF16)
                 nc.sync.dma_start(out=h_tile[:].rearrange("q (u e) n -> q u e n", u=2), in_=h_v[b])
                 h_raw[b] = h_tile
 
         def load_feat(i):
-            if i < TOTAL:
-                feat_tile = feats.tile([P, ROWS, N], BF16)
-                nc.sync.dma_start(out=feat_tile[:], in_=feat_v[i])
-                feat_sb[i] = feat_tile
+            feat_tile = feats.tile([P, ROWS, N], BF16)
+            nc.sync.dma_start(out=feat_tile[:], in_=feat_v[i])
+            feat_sb[i] = feat_tile
 
-        def regroup(i):
+        def quantise_operands(i):
             b, s = divmod(i, SLABS)
             if b == 0:
                 w_words = w_raw[s][:].rearrange("p j k -> p (j k)").bitcast(F32)
                 w_group = grouped.tile([P, ROWS * P * PACK], BF16, align_bytes=64)
                 w_group_words = w_group[:].bitcast(F32).rearrange("q (j p u) -> q j p u", j=ROWS, u=2)
                 for half in range(2):
-                    w_t = psum_t.tile([P, 2, 2, P], F32)
+                    w_t = psum_aux.tile([P, 2, 2, P], F32, tag="aux")
                     for jj in range(2):
                         for u in range(2):
                             first = ((2 * half + jj) * 2 + u) * P
@@ -128,31 +114,28 @@ def tile_crossattention_pa_kernel(tc, feat, h_attn, w_out, b_out, gamma, beta, o
                         out=w_group_words[:, 2 * half : 2 * half + 2],
                         in_=w_t[:].rearrange("q jj u p -> q jj p u"),
                     )
-                w_grouped[s] = w_group
             if s == 0:
                 h_group = grouped.tile([P, N, PACK], BF16, align_bytes=64)
                 nc.vector.tensor_copy(
                     out=h_group[:].rearrange("q (c i) t -> q c t i", i=4),
                     in_=h_raw[b][:].rearrange("q t (c i) -> q c t i", i=4),
                 )
-                h_grouped[b] = h_group
-
-        def quantise(i):
-            b, s = divmod(i, SLABS)
             if b == 0:
                 nc.vector.quantize_mx(
-                    out=w_codes[:, s, :].bitcast(FP8X4), scales=w_scales[:, s, :], in_=w_grouped[s][:]
+                    out=w_codes[:, s, :].bitcast(FP8X4), scales=w_scales[:, s, :], in_=w_group[:]
                 )
             if s == 0:
                 nc.vector.quantize_mx(
                     out=h_codes[:, b, :].bitcast(FP8X4),
                     scales=h_scales[:, b, :],
-                    in_=h_grouped[b][:].rearrange("q n t -> q (n t)"),
+                    in_=h_group[:].rearrange("q n t -> q (n t)"),
                 )
 
-        def project(i, half):
+        def slab(i):
             b, s = divmod(i, SLABS)
-            for j in range(half * HALF, (half + 1) * HALF):
+            x = xs.tile([P, ROWS, N], F32)
+            sums = small.tile([P, ROWS], F32)
+            for j in range(ROWS):
                 y = psum_y.tile([P, N], F32)
                 cols = slice(j * P, (j + 1) * P)
                 nc.tensor.matmul_mx(
@@ -164,143 +147,75 @@ def tile_crossattention_pa_kernel(tc, feat, h_attn, w_out, b_out, gamma, beta, o
                     start=True,
                     stop=True,
                 )
-                y_ps[(i, j)] = y
-
-        def residual(i, half):
-            s = i % SLABS
-            if half == 0:
-                x = xs.tile([P, ROWS, N], F32)
-                x_sb[i] = x
-                sums = small.tile([P, 2, HALF + 1, 8], F32)
-                sums_sb[i] = sums
-            for r in range(HALF):
-                j = half * HALF + r
                 nc.vector.scalar_tensor_tensor(
-                    out=x_sb[i][:, j, :],
-                    in0=y_ps[(i, j)][:],
+                    out=x[:, j, :],
+                    in0=y[:],
                     scalar=params[:, 0, s, j : j + 1],
                     in1=feat_sb[i][:, j, :],
                     op0=ALU.add,
                     op1=ALU.add,
-                    accum_out=sums_sb[i][:, half, r, 0:1],
+                    accum_out=sums[:, j : j + 1],
                 )
 
-        def squares(i, half):
-            sq = junk.tile([P, HALF * N], BF16)
+            mom = psum_aux.tile([P, ROWS + 1], F32, tag="aux")
+            nc.tensor.matmul(out=mom[:, 0:ROWS], lhsT=group_avg[:], rhs=sums[:], start=True, stop=True)
+            neg_mean = small.tile([P, 1], F32)
+            nc.vector.tensor_reduce(out=neg_mean[:], in_=mom[:, 0:ROWS], axis=AX.X, op=ALU.add)
+
+            sq = junk.tile([P, ROWS * N], BF16)
+            sum_sq = small.tile([P, 1], F32)
             nc.scalar.activation(
                 out=sq[:],
-                in_=x_sb[i][:, half * HALF : (half + 1) * HALF, :].rearrange("p j n -> p (j n)"),
+                in_=x[:].rearrange("p j n -> p (j n)"),
                 func=ACT.Square,
-                accum_out=sums_sb[i][:, half, HALF, 0:1],
+                bias=neg_mean[:, 0:1],
+                accum_out=sum_sq[:, 0:1],
             )
-            if half == 0:
-                mom = psum_s.tile([P, HALF + 1], F32)
-                mom_ps[i] = mom
             nc.tensor.matmul(
-                out=mom_ps[i][:],
-                lhsT=group_avg[:],
-                rhs=sums_sb[i][:, half, :, 0],
-                start=(half == 0),
-                stop=(half == 1),
+                out=mom[:, ROWS : ROWS + 1], lhsT=group_avg[:], rhs=sum_sq[:], start=True, stop=True
             )
-
-        def moments(i):
-            mom = mom_ps[i]
-            neg_mean = small.tile([P, 1], F32)
-            nc.vector.tensor_reduce(out=neg_mean[:], in_=mom[:, 0:HALF], axis=AX.X, op=ALU.add)
-            neg_var = small.tile([P, 1], F32)
-            nc.vector.scalar_tensor_tensor(
-                out=neg_var[:],
-                in0=neg_mean[:],
-                scalar=neg_mean[:, 0:1],
-                in1=mom[:, HALF : HALF + 1],
-                op0=ALU.mult,
-                op1=ALU.add,
-            )
-            neg_mean_sb[i] = neg_mean
-            neg_var_sb[i] = neg_var
-
-        def inv_std(i):
             rstd = small.tile([P, 1], F32)
             nc.scalar.activation(
-                out=rstd[:], in_=neg_var_sb[i][:], func=ACT.Abs_reciprocal_sqrt, bias=eps[:, 0:1], scale=-1.0
+                out=rstd[:], in_=mom[:, ROWS : ROWS + 1], func=ACT.Abs_reciprocal_sqrt, bias=eps[:, 0:1], scale=-1.0
             )
-            rstd_sb[i] = rstd
+            neg_mean_rstd = small.tile([P, 1], F32)
+            nc.scalar.activation(out=neg_mean_rstd[:], in_=rstd[:], func=ACT.Copy, scale=neg_mean[:, 0:1])
 
-        def affine(i):
-            s = i % SLABS
             gain = small.tile([P, ROWS], F32)
             nc.vector.tensor_scalar(
-                out=gain[:], in0=params[:, 1, s, :], scalar1=rstd_sb[i][:, 0:1], scalar2=None, op0=ALU.mult
+                out=gain[:], in0=params[:, 1, s, :], scalar1=rstd[:, 0:1], scalar2=None, op0=ALU.mult
             )
             shift = small.tile([P, ROWS], F32)
             nc.vector.scalar_tensor_tensor(
                 out=shift[:],
-                in0=gain[:],
-                scalar=neg_mean_sb[i][:, 0:1],
+                in0=params[:, 1, s, :],
+                scalar=neg_mean_rstd[:, 0:1],
                 in1=params[:, 2, s, :],
                 op0=ALU.mult,
                 op1=ALU.add,
             )
-            gain_sb[i] = gain
-            shift_sb[i] = shift
-
-        def normalise(i):
-            x = x_sb[i]
             helper = nc.vector if i == TOTAL - 1 else nc.gpsimd
             for j in range(ROWS):
-                gain_j = gain_sb[i][:, j : j + 1]
-                shift_j = shift_sb[i][:, j : j + 1]
-                if j < ROWS_ON_SCALAR:
-                    nc.scalar.activation(out=x[:, j, :], in_=x[:, j, :], func=ACT.Identity, bias=shift_j, scale=gain_j)
-                else:
-                    helper.tensor_scalar(
-                        out=x[:, j, :], in0=x[:, j, :], scalar1=gain_j, scalar2=shift_j, op0=ALU.mult, op1=ALU.add
-                    )
+                gain_j = gain[:, j : j + 1]
+                shift_j = shift[:, j : j + 1]
+                engine = nc.vector if j < ROWS_ON_VECTOR else helper
+                engine.tensor_scalar(
+                    out=x[:, j, :], in0=x[:, j, :], scalar1=gain_j, scalar2=shift_j, op0=ALU.mult, op1=ALU.add
+                )
             for half in range(2):
                 rows = slice(half * HALF, (half + 1) * HALF)
                 nc.sync.dma_start(out=out_v[i][:, rows, :], in_=x[:, rows, :])
 
-
         load_operands(0)
         load_operands(1)
-        for i in range(AHEAD):
+        for i in range(TOTAL):
             load_feat(i)
-            load_operands(i + 2)
+            if i + 2 < TOTAL:
+                load_operands(i + 2)
 
-        regroup(0)
-        regroup(1)
-        quantise(0)
+        quantise_operands(0)
         nc.vector.tensor_copy(out=params[:], in_=params_bf[:])
-        project(0, 0)
-        project(0, 1)
-
-        for step in range(TOTAL + 1):
-            here = step < TOTAL
-            before = step >= 1
-            after = step + 1 < TOTAL
-            load_feat(step + AHEAD)
-            load_operands(step + AHEAD + 2)
-            if step + 2 < TOTAL:
-                regroup(step + 2)
-            if here:
-                residual(step, 0)
-            if before:
-                moments(step - 1)
-            if after:
-                quantise(step + 1)
-                project(step + 1, 0)
-            if here:
-                squares(step, 0)
-            if before:
-                inv_std(step - 1)
-            if here:
-                residual(step, 1)
-            if after:
-                project(step + 1, 1)
-            if before:
-                affine(step - 1)
-            if here:
-                squares(step, 1)
-            if before:
-                normalise(step - 1)
+        for i in range(TOTAL):
+            if i + 1 < TOTAL:
+                quantise_operands(i + 1)
+            slab(i)

@@ -30,7 +30,9 @@ QUADRANT = GROUP // ROWS
 FLOPS = 2 * BATCH * CHANNELS * K * N
 
 HALF = ROWS // 2
-ROWS_ON_VECTOR = 1
+ROWS_ON_SCALAR = 1
+LAG = 2
+AHEAD = 16
 
 
 def tile_crossattention_pa_kernel(tc, feat, h_attn, w_out, b_out, gamma, beta, out):
@@ -45,12 +47,14 @@ def tile_crossattention_pa_kernel(tc, feat, h_attn, w_out, b_out, gamma, beta, o
         const = ctx.enter_context(tc.tile_pool(name="const", bufs=1))
         raw = ctx.enter_context(tc.tile_pool(name="raw", bufs=4))
         grouped = ctx.enter_context(tc.tile_pool(name="grouped", bufs=2))
-        feats = ctx.enter_context(tc.tile_pool(name="feats", bufs=TOTAL))
-        xs = ctx.enter_context(tc.tile_pool(name="xs", bufs=8))
-        junk = ctx.enter_context(tc.tile_pool(name="junk", bufs=2))
+        feats = ctx.enter_context(tc.tile_pool(name="feats", bufs=16))
+        xs = ctx.enter_context(tc.tile_pool(name="xs", bufs=9))
+        junk = ctx.enter_context(tc.tile_pool(name="junk", bufs=3))
         small = ctx.enter_context(tc.tile_pool(name="small", bufs=4))
         psum_y = ctx.enter_context(tc.psum_pool(name="psum_y", bufs=4))
-        psum_aux = ctx.enter_context(tc.psum_pool(name="psum_aux", bufs=4))
+        psum_const = ctx.enter_context(tc.psum_pool(name="psum_const", bufs=1))
+        psum_t = ctx.enter_context(tc.psum_pool(name="psum_t", bufs=2))
+        psum_s = ctx.enter_context(tc.psum_pool(name="psum_s", bufs=1))
 
         eps = const.tile([P, 1], F32)
         nc.vector.memset(eps[:], EPS)
@@ -80,32 +84,44 @@ def tile_crossattention_pa_kernel(tc, feat, h_attn, w_out, b_out, gamma, beta, o
 
         h_raw = {}
         w_raw = {}
+        h_grouped = {}
+        w_grouped = {}
         feat_sb = {}
+        y_ps = {}
+        x_sb = {}
+        sums_sb = {}
+        mom_ps = {}
+        neg_mean_sb = {}
+        neg_var_sb = {}
+        rstd_sb = {}
+        gain_sb = {}
+        shift_sb = {}
 
         def load_operands(i):
             b, s = divmod(i, SLABS)
-            if b == 0:
+            if i < TOTAL and b == 0:
                 w_tile = raw.tile([P, ROWS, K], BF16)
                 nc.sync.dma_start(out=w_tile[:], in_=w_v[s])
                 w_raw[s] = w_tile
-            if s == 0:
+            if i < TOTAL and s == 0:
                 h_tile = raw.tile([P, PACK, N], BF16)
                 nc.sync.dma_start(out=h_tile[:].rearrange("q (u e) n -> q u e n", u=2), in_=h_v[b])
                 h_raw[b] = h_tile
 
         def load_feat(i):
-            feat_tile = feats.tile([P, ROWS, N], BF16)
-            nc.sync.dma_start(out=feat_tile[:], in_=feat_v[i])
-            feat_sb[i] = feat_tile
+            if i < TOTAL:
+                feat_tile = feats.tile([P, ROWS, N], BF16)
+                nc.sync.dma_start(out=feat_tile[:], in_=feat_v[i])
+                feat_sb[i] = feat_tile
 
-        def quantise_operands(i):
+        def regroup(i):
             b, s = divmod(i, SLABS)
             if b == 0:
                 w_words = w_raw[s][:].rearrange("p j k -> p (j k)").bitcast(F32)
                 w_group = grouped.tile([P, ROWS * P * PACK], BF16, align_bytes=64)
                 w_group_words = w_group[:].bitcast(F32).rearrange("q (j p u) -> q j p u", j=ROWS, u=2)
                 for half in range(2):
-                    w_t = psum_aux.tile([P, 2, 2, P], F32, tag="aux")
+                    w_t = psum_t.tile([P, 2, 2, P], F32)
                     for jj in range(2):
                         for u in range(2):
                             first = ((2 * half + jj) * 2 + u) * P
@@ -114,108 +130,190 @@ def tile_crossattention_pa_kernel(tc, feat, h_attn, w_out, b_out, gamma, beta, o
                         out=w_group_words[:, 2 * half : 2 * half + 2],
                         in_=w_t[:].rearrange("q jj u p -> q jj p u"),
                     )
+                w_grouped[s] = w_group
             if s == 0:
                 h_group = grouped.tile([P, N, PACK], BF16, align_bytes=64)
                 nc.vector.tensor_copy(
                     out=h_group[:].rearrange("q (c i) t -> q c t i", i=4),
                     in_=h_raw[b][:].rearrange("q t (c i) -> q c t i", i=4),
                 )
+                h_grouped[b] = h_group
+
+        def quantise(i):
+            b, s = divmod(i, SLABS)
             if b == 0:
                 nc.vector.quantize_mx(
-                    out=w_codes[:, s, :].bitcast(FP8X4), scales=w_scales[:, s, :], in_=w_group[:]
+                    out=w_codes[:, s, :].bitcast(FP8X4), scales=w_scales[:, s, :], in_=w_grouped[s][:]
                 )
             if s == 0:
                 nc.vector.quantize_mx(
                     out=h_codes[:, b, :].bitcast(FP8X4),
                     scales=h_scales[:, b, :],
-                    in_=h_group[:].rearrange("q n t -> q (n t)"),
+                    in_=h_grouped[b][:].rearrange("q n t -> q (n t)"),
                 )
 
-        def slab(i):
+        def project(i, j):
             b, s = divmod(i, SLABS)
-            x = xs.tile([P, ROWS, N], F32)
-            sums = small.tile([P, ROWS], F32)
-            for j in range(ROWS):
-                y = psum_y.tile([P, N], F32)
-                cols = slice(j * P, (j + 1) * P)
-                nc.tensor.matmul_mx(
-                    out=y[:],
-                    lhsT=w_codes[:, s, cols].bitcast(FP8X4),
-                    lhsT_scale=w_scales[:, s, cols],
-                    rhs=h_codes[:, b, :].bitcast(FP8X4),
-                    rhs_scale=h_scales[:, b, :],
-                    start=True,
-                    stop=True,
-                )
-                nc.vector.scalar_tensor_tensor(
-                    out=x[:, j, :],
-                    in0=y[:],
-                    scalar=params[:, 0, s, j : j + 1],
-                    in1=feat_sb[i][:, j, :],
-                    op0=ALU.add,
-                    op1=ALU.add,
-                    accum_out=sums[:, j : j + 1],
-                )
+            y = psum_y.tile([P, N], F32)
+            cols = slice(j * P, (j + 1) * P)
+            nc.tensor.matmul_mx(
+                out=y[:],
+                lhsT=w_codes[:, s, cols].bitcast(FP8X4),
+                lhsT_scale=w_scales[:, s, cols],
+                rhs=h_codes[:, b, :].bitcast(FP8X4),
+                rhs_scale=h_scales[:, b, :],
+                start=True,
+                stop=True,
+            )
+            y_ps[(i, j)] = y
 
-            mom = psum_aux.tile([P, ROWS + 1], F32, tag="aux")
-            nc.tensor.matmul(out=mom[:, 0:ROWS], lhsT=group_avg[:], rhs=sums[:], start=True, stop=True)
-            neg_mean = small.tile([P, 1], F32)
-            nc.vector.tensor_reduce(out=neg_mean[:], in_=mom[:, 0:ROWS], axis=AX.X, op=ALU.add)
+        def residual(i, j):
+            s = i % SLABS
+            half, r = divmod(j, HALF)
+            if j == 0:
+                x = xs.tile([P, ROWS, N], F32)
+                x_sb[i] = x
+                sums = small.tile([P, 2, HALF + 1, 8], F32)
+                sums_sb[i] = sums
+            nc.vector.scalar_tensor_tensor(
+                out=x_sb[i][:, j, :],
+                in0=y_ps[(i, j)][:],
+                scalar=params[:, 0, s, j : j + 1],
+                in1=feat_sb[i][:, j, :],
+                op0=ALU.add,
+                op1=ALU.add,
+                accum_out=sums_sb[i][:, half, r, 0:1],
+            )
 
-            sq = junk.tile([P, ROWS * N], BF16)
-            sum_sq = small.tile([P, 1], F32)
+        def squares(i, half):
+            sq = junk.tile([P, HALF * N], BF16)
             nc.scalar.activation(
                 out=sq[:],
-                in_=x[:].rearrange("p j n -> p (j n)"),
+                in_=x_sb[i][:, half * HALF : (half + 1) * HALF, :].rearrange("p j n -> p (j n)"),
                 func=ACT.Square,
-                bias=neg_mean[:, 0:1],
-                accum_out=sum_sq[:, 0:1],
+                accum_out=sums_sb[i][:, half, HALF, 0:1],
             )
+            if half == 0:
+                mom = psum_s.tile([P, HALF + 1], F32)
+                mom_ps[i] = mom
             nc.tensor.matmul(
-                out=mom[:, ROWS : ROWS + 1], lhsT=group_avg[:], rhs=sum_sq[:], start=True, stop=True
+                out=mom_ps[i][:],
+                lhsT=group_avg[:],
+                rhs=sums_sb[i][:, half, :, 0],
+                start=(half == 0),
+                stop=(half == 1),
             )
-            rstd = small.tile([P, 1], F32)
-            nc.scalar.activation(
-                out=rstd[:], in_=mom[:, ROWS : ROWS + 1], func=ACT.Abs_reciprocal_sqrt, bias=eps[:, 0:1], scale=-1.0
-            )
-            neg_mean_rstd = small.tile([P, 1], F32)
-            nc.scalar.activation(out=neg_mean_rstd[:], in_=rstd[:], func=ACT.Copy, scale=neg_mean[:, 0:1])
 
-            gain = small.tile([P, ROWS], F32)
-            nc.vector.tensor_scalar(
-                out=gain[:], in0=params[:, 1, s, :], scalar1=rstd[:, 0:1], scalar2=None, op0=ALU.mult
-            )
-            shift = small.tile([P, ROWS], F32)
+        def mean(i):
+            neg_mean = small.tile([P, 1], F32)
+            nc.vector.tensor_reduce(out=neg_mean[:], in_=mom_ps[i][:, 0:HALF], axis=AX.X, op=ALU.add)
+            neg_mean_sb[i] = neg_mean
+
+        def variance(i):
+            neg_var = small.tile([P, 1], F32)
             nc.vector.scalar_tensor_tensor(
-                out=shift[:],
-                in0=params[:, 1, s, :],
-                scalar=neg_mean_rstd[:, 0:1],
-                in1=params[:, 2, s, :],
+                out=neg_var[:],
+                in0=neg_mean_sb[i][:],
+                scalar=neg_mean_sb[i][:, 0:1],
+                in1=mom_ps[i][:, HALF : HALF + 1],
                 op0=ALU.mult,
                 op1=ALU.add,
             )
-            helper = nc.vector if i == TOTAL - 1 else nc.gpsimd
+            neg_var_sb[i] = neg_var
+
+        def inv_std(i):
+            rstd = small.tile([P, 1], F32)
+            nc.scalar.activation(
+                out=rstd[:], in_=neg_var_sb[i][:], func=ACT.Abs_reciprocal_sqrt, bias=eps[:, 0:1], scale=-1.0
+            )
+            rstd_sb[i] = rstd
+
+        def make_gain(i):
+            s = i % SLABS
+            gain = small.tile([P, ROWS], F32)
+            nc.vector.tensor_scalar(
+                out=gain[:], in0=affine_ps[:, 0, s, :], scalar1=rstd_sb[i][:, 0:1], scalar2=None, op0=ALU.mult
+            )
+            gain_sb[i] = gain
+
+        def make_shift(i):
+            s = i % SLABS
+            shift = small.tile([P, ROWS], F32)
+            nc.vector.scalar_tensor_tensor(
+                out=shift[:],
+                in0=gain_sb[i][:],
+                scalar=neg_mean_sb[i][:, 0:1],
+                in1=affine_ps[:, 1, s, :],
+                op0=ALU.mult,
+                op1=ALU.add,
+            )
+            shift_sb[i] = shift
+
+        def normalise(i):
+            x = x_sb[i]
+            helper = nc.vector if i >= TOTAL - LAG else nc.gpsimd
             for j in range(ROWS):
-                gain_j = gain[:, j : j + 1]
-                shift_j = shift[:, j : j + 1]
-                engine = nc.vector if j < ROWS_ON_VECTOR else helper
-                engine.tensor_scalar(
-                    out=x[:, j, :], in0=x[:, j, :], scalar1=gain_j, scalar2=shift_j, op0=ALU.mult, op1=ALU.add
-                )
+                gain_j = gain_sb[i][:, j : j + 1]
+                shift_j = shift_sb[i][:, j : j + 1]
+                if j < ROWS_ON_SCALAR:
+                    nc.scalar.activation(out=x[:, j, :], in_=x[:, j, :], func=ACT.Identity, bias=shift_j, scale=gain_j)
+                else:
+                    helper.tensor_scalar(
+                        out=x[:, j, :], in0=x[:, j, :], scalar1=gain_j, scalar2=shift_j, op0=ALU.mult, op1=ALU.add
+                    )
             for half in range(2):
                 rows = slice(half * HALF, (half + 1) * HALF)
                 nc.sync.dma_start(out=out_v[i][:, rows, :], in_=x[:, rows, :])
 
+        ctx.enter_context(tc.manual_schedule())
+
         load_operands(0)
         load_operands(1)
-        for i in range(TOTAL):
+        for i in range(AHEAD):
             load_feat(i)
-            if i + 2 < TOTAL:
-                load_operands(i + 2)
+            load_operands(i + 2)
 
-        quantise_operands(0)
+        regroup(0)
+        regroup(1)
+        quantise(0)
         nc.vector.tensor_copy(out=params[:], in_=params_bf[:])
-        for i in range(TOTAL):
-            if i + 1 < TOTAL:
-                quantise_operands(i + 1)
-            slab(i)
+        for j in range(ROWS):
+            project(0, j)
+        affine_ps = psum_const.tile([P, 2, SLABS, ROWS], F32)
+        nc.tensor.matmul(
+            out=affine_ps[:].rearrange("p a s j -> p (a s j)"),
+            lhsT=ident[:],
+            rhs=params[:, 1:3].rearrange("p a s j -> p (a s j)"),
+            start=True,
+            stop=True,
+        )
+
+        for step in range(TOTAL + LAG):
+            here = step < TOTAL
+            after = step + 1 < TOTAL
+            stats = 1 <= step <= TOTAL
+            finish = step >= LAG
+            if after:
+                quantise(step + 1)
+            if step + 2 < TOTAL:
+                regroup(step + 2)
+            for j in range(ROWS):
+                if here:
+                    residual(step, j)
+                if after:
+                    project(step + 1, j)
+                if j == ROWS - 2 and stats:
+                    mean(step - 1)
+                if j == ROWS - 2 and finish:
+                    make_gain(step - LAG)
+                if j == ROWS - 1 and stats:
+                    variance(step - 1)
+                if j == ROWS - 1 and finish:
+                    make_shift(step - LAG)
+            for half in range(2):
+                if here:
+                    squares(step, half)
+            if stats:
+                inv_std(step - 1)
+            if finish:
+                normalise(step - LAG)

@@ -16,23 +16,22 @@ P = 128
 PACK = 4
 BATCH = 4
 CHANNELS = 2048
-K = 512
+K = P * PACK
 N = 512
 GROUP = 128
 EPS = 1e-5
 
 ROWS = 4
+HALF = ROWS // 2
 SLAB = P * ROWS
 SLABS = CHANNELS // SLAB
 TOTAL = BATCH * SLABS
 QUADRANT = GROUP // ROWS
+LAG = 2
+ROWS_ON_SCALAR = 1
+BLOCK = 8
 
 FLOPS = 2 * BATCH * CHANNELS * K * N
-
-HALF = ROWS // 2
-ROWS_ON_SCALAR = 1
-LAG = 2
-AHEAD = 16
 
 
 def tile_crossattention_pa_kernel(tc, feat, h_attn, w_out, b_out, gamma, beta, out):
@@ -45,16 +44,16 @@ def tile_crossattention_pa_kernel(tc, feat, h_attn, w_out, b_out, gamma, beta, o
 
     with ExitStack() as ctx:
         const = ctx.enter_context(tc.tile_pool(name="const", bufs=1))
-        raw = ctx.enter_context(tc.tile_pool(name="raw", bufs=4))
+        raw = ctx.enter_context(tc.tile_pool(name="raw", bufs=SLABS))
+        feats = ctx.enter_context(tc.tile_pool(name="feats", bufs=TOTAL))
         grouped = ctx.enter_context(tc.tile_pool(name="grouped", bufs=2))
-        feats = ctx.enter_context(tc.tile_pool(name="feats", bufs=16))
         xs = ctx.enter_context(tc.tile_pool(name="xs", bufs=9))
-        junk = ctx.enter_context(tc.tile_pool(name="junk", bufs=3))
-        small = ctx.enter_context(tc.tile_pool(name="small", bufs=4))
-        psum_y = ctx.enter_context(tc.psum_pool(name="psum_y", bufs=4))
-        psum_const = ctx.enter_context(tc.psum_pool(name="psum_const", bufs=1))
+        scratch = ctx.enter_context(tc.tile_pool(name="scratch", bufs=3))
+        small = ctx.enter_context(tc.tile_pool(name="small", bufs=LAG + 2))
+        psum_y = ctx.enter_context(tc.psum_pool(name="psum_y", bufs=ROWS))
         psum_t = ctx.enter_context(tc.psum_pool(name="psum_t", bufs=2))
         psum_s = ctx.enter_context(tc.psum_pool(name="psum_s", bufs=1))
+        psum_const = ctx.enter_context(tc.psum_pool(name="psum_const", bufs=1))
 
         eps = const.tile([P, 1], F32)
         nc.vector.memset(eps[:], EPS)
@@ -67,8 +66,8 @@ def tile_crossattention_pa_kernel(tc, feat, h_attn, w_out, b_out, gamma, beta, o
         group_avg = const.tile([P, P], F32)
         nc.vector.memset(group_avg[:], 0.0)
         for g in range(P // QUADRANT):
-            rows = slice(g * QUADRANT, (g + 1) * QUADRANT)
-            nc.vector.memset(group_avg[rows, rows], -1.0 / (GROUP * N))
+            quadrant = slice(g * QUADRANT, (g + 1) * QUADRANT)
+            nc.vector.memset(group_avg[quadrant, quadrant], -1.0 / (GROUP * N))
 
         params_bf = const.tile([P, 3, SLABS, ROWS], BF16)
         for which, vec in enumerate((b_out, gamma, beta)):
@@ -82,10 +81,10 @@ def tile_crossattention_pa_kernel(tc, feat, h_attn, w_out, b_out, gamma, beta, o
         h_codes = const.tile([P, BATCH, N], U32, align_bytes=64)
         h_scales = const.tile([P, BATCH, N], U8, align_bytes=64)
 
-        h_raw = {}
         w_raw = {}
-        h_grouped = {}
+        h_raw = {}
         w_grouped = {}
+        h_grouped = {}
         feat_sb = {}
         y_ps = {}
         x_sb = {}
@@ -97,41 +96,46 @@ def tile_crossattention_pa_kernel(tc, feat, h_attn, w_out, b_out, gamma, beta, o
         gain_sb = {}
         shift_sb = {}
 
+        def new_operands(i):
+            b, s = divmod(i, SLABS)
+            return i < TOTAL and b == 0, i < TOTAL and s == 0
+
         def load_operands(i):
             b, s = divmod(i, SLABS)
-            if i < TOTAL and b == 0:
+            new_w, new_h = new_operands(i)
+            if new_w:
                 w_tile = raw.tile([P, ROWS, K], BF16)
                 nc.sync.dma_start(out=w_tile[:], in_=w_v[s])
                 w_raw[s] = w_tile
-            if i < TOTAL and s == 0:
+            if new_h:
                 h_tile = raw.tile([P, PACK, N], BF16)
                 nc.sync.dma_start(out=h_tile[:].rearrange("q (u e) n -> q u e n", u=2), in_=h_v[b])
                 h_raw[b] = h_tile
 
         def load_feat(i):
-            if i < TOTAL:
-                feat_tile = feats.tile([P, ROWS, N], BF16)
-                nc.sync.dma_start(out=feat_tile[:], in_=feat_v[i])
-                feat_sb[i] = feat_tile
+            feat_tile = feats.tile([P, ROWS, N], BF16)
+            nc.sync.dma_start(out=feat_tile[:], in_=feat_v[i])
+            feat_sb[i] = feat_tile
 
         def regroup(i):
             b, s = divmod(i, SLABS)
-            if b == 0:
+            new_w, new_h = new_operands(i)
+            if new_w:
                 w_words = w_raw[s][:].rearrange("p j k -> p (j k)").bitcast(F32)
                 w_group = grouped.tile([P, ROWS * P * PACK], BF16, align_bytes=64)
                 w_group_words = w_group[:].bitcast(F32).rearrange("q (j p u) -> q j p u", j=ROWS, u=2)
                 for half in range(2):
-                    w_t = psum_t.tile([P, 2, 2, P], F32)
-                    for jj in range(2):
+                    w_t = psum_t.tile([P, HALF, 2, P], F32)
+                    for r in range(HALF):
                         for u in range(2):
-                            first = ((2 * half + jj) * 2 + u) * P
-                            nc.tensor.transpose(w_t[:, jj, u, :], w_words[:, first : first + P], ident[:])
+                            first = ((half * HALF + r) * 2 + u) * P
+                            nc.tensor.transpose(w_t[:, r, u, :], w_words[:, first : first + P], ident[:])
                     nc.scalar.copy(
-                        out=w_group_words[:, 2 * half : 2 * half + 2],
-                        in_=w_t[:].rearrange("q jj u p -> q jj p u"),
+                        out=w_group_words[:, half * HALF : (half + 1) * HALF],
+                        in_=w_t[:].rearrange("q r u p -> q r p u"),
                     )
                 w_grouped[s] = w_group
-            if s == 0:
+            if new_h:
                 h_group = grouped.tile([P, N, PACK], BF16, align_bytes=64)
                 nc.vector.tensor_copy(
                     out=h_group[:].rearrange("q (c i) t -> q c t i", i=4),
@@ -141,11 +145,12 @@ def tile_crossattention_pa_kernel(tc, feat, h_attn, w_out, b_out, gamma, beta, o
 
         def quantise(i):
             b, s = divmod(i, SLABS)
-            if b == 0:
+            new_w, new_h = new_operands(i)
+            if new_w:
                 nc.vector.quantize_mx(
                     out=w_codes[:, s, :].bitcast(FP8X4), scales=w_scales[:, s, :], in_=w_grouped[s][:]
                 )
-            if s == 0:
+            if new_h:
                 nc.vector.quantize_mx(
                     out=h_codes[:, b, :].bitcast(FP8X4),
                     scales=h_scales[:, b, :],
@@ -153,6 +158,8 @@ def tile_crossattention_pa_kernel(tc, feat, h_attn, w_out, b_out, gamma, beta, o
                 )
 
         def project(i, j):
+            if i >= TOTAL:
+                return
             b, s = divmod(i, SLABS)
             y = psum_y.tile([P, N], F32)
             cols = slice(j * P, (j + 1) * P)
@@ -168,12 +175,14 @@ def tile_crossattention_pa_kernel(tc, feat, h_attn, w_out, b_out, gamma, beta, o
             y_ps[(i, j)] = y
 
         def residual(i, j):
+            if i >= TOTAL:
+                return
             s = i % SLABS
             half, r = divmod(j, HALF)
             if j == 0:
                 x = xs.tile([P, ROWS, N], F32)
                 x_sb[i] = x
-                sums = small.tile([P, 2, HALF + 1, 8], F32)
+                sums = small.tile([P, 2, HALF + 1, BLOCK], F32)
                 sums_sb[i] = sums
             nc.vector.scalar_tensor_tensor(
                 out=x_sb[i][:, j, :],
@@ -186,7 +195,9 @@ def tile_crossattention_pa_kernel(tc, feat, h_attn, w_out, b_out, gamma, beta, o
             )
 
         def squares(i, half):
-            sq = junk.tile([P, HALF * N], BF16)
+            if i >= TOTAL:
+                return
+            sq = scratch.tile([P, HALF * N], BF16)
             nc.scalar.activation(
                 out=sq[:],
                 in_=x_sb[i][:, half * HALF : (half + 1) * HALF, :].rearrange("p j n -> p (j n)"),
@@ -205,11 +216,15 @@ def tile_crossattention_pa_kernel(tc, feat, h_attn, w_out, b_out, gamma, beta, o
             )
 
         def mean(i):
+            if not 0 <= i < TOTAL:
+                return
             neg_mean = small.tile([P, 1], F32)
             nc.vector.tensor_reduce(out=neg_mean[:], in_=mom_ps[i][:, 0:HALF], axis=AX.X, op=ALU.add)
             neg_mean_sb[i] = neg_mean
 
         def variance(i):
+            if not 0 <= i < TOTAL:
+                return
             neg_var = small.tile([P, 1], F32)
             nc.vector.scalar_tensor_tensor(
                 out=neg_var[:],
@@ -222,6 +237,8 @@ def tile_crossattention_pa_kernel(tc, feat, h_attn, w_out, b_out, gamma, beta, o
             neg_var_sb[i] = neg_var
 
         def inv_std(i):
+            if not 0 <= i < TOTAL:
+                return
             rstd = small.tile([P, 1], F32)
             nc.scalar.activation(
                 out=rstd[:], in_=neg_var_sb[i][:], func=ACT.Abs_reciprocal_sqrt, bias=eps[:, 0:1], scale=-1.0
@@ -229,27 +246,31 @@ def tile_crossattention_pa_kernel(tc, feat, h_attn, w_out, b_out, gamma, beta, o
             rstd_sb[i] = rstd
 
         def make_gain(i):
-            s = i % SLABS
+            if not 0 <= i < TOTAL:
+                return
             gain = small.tile([P, ROWS], F32)
             nc.vector.tensor_scalar(
-                out=gain[:], in0=affine_ps[:, 0, s, :], scalar1=rstd_sb[i][:, 0:1], scalar2=None, op0=ALU.mult
+                out=gain[:], in0=gamma_of[:, i % SLABS, :], scalar1=rstd_sb[i][:, 0:1], scalar2=None, op0=ALU.mult
             )
             gain_sb[i] = gain
 
         def make_shift(i):
-            s = i % SLABS
+            if not 0 <= i < TOTAL:
+                return
             shift = small.tile([P, ROWS], F32)
             nc.vector.scalar_tensor_tensor(
                 out=shift[:],
                 in0=gain_sb[i][:],
                 scalar=neg_mean_sb[i][:, 0:1],
-                in1=affine_ps[:, 1, s, :],
+                in1=beta_of[:, i % SLABS, :],
                 op0=ALU.mult,
                 op1=ALU.add,
             )
             shift_sb[i] = shift
 
         def normalise(i):
+            if not 0 <= i < TOTAL:
+                return
             x = x_sb[i]
             helper = nc.vector if i >= TOTAL - LAG else nc.gpsimd
             for j in range(ROWS):
@@ -269,7 +290,7 @@ def tile_crossattention_pa_kernel(tc, feat, h_attn, w_out, b_out, gamma, beta, o
 
         load_operands(0)
         load_operands(1)
-        for i in range(AHEAD):
+        for i in range(TOTAL):
             load_feat(i)
             load_operands(i + 2)
 
@@ -287,33 +308,25 @@ def tile_crossattention_pa_kernel(tc, feat, h_attn, w_out, b_out, gamma, beta, o
             start=True,
             stop=True,
         )
+        gamma_of = affine_ps[:, 0]
+        beta_of = affine_ps[:, 1]
 
         for step in range(TOTAL + LAG):
-            here = step < TOTAL
-            after = step + 1 < TOTAL
-            stats = 1 <= step <= TOTAL
-            finish = step >= LAG
-            if after:
-                quantise(step + 1)
-            if step + 2 < TOTAL:
-                regroup(step + 2)
-            for j in range(ROWS):
-                if here:
-                    residual(step, j)
-                if after:
-                    project(step + 1, j)
-                if j == ROWS - 2 and stats:
-                    mean(step - 1)
-                if j == ROWS - 2 and finish:
-                    make_gain(step - LAG)
-                if j == ROWS - 1 and stats:
-                    variance(step - 1)
-                if j == ROWS - 1 and finish:
-                    make_shift(step - LAG)
-            for half in range(2):
-                if here:
-                    squares(step, half)
-            if stats:
-                inv_std(step - 1)
-            if finish:
-                normalise(step - LAG)
+            regroup(step + 2)
+            residual(step, 0)
+            residual(step, 1)
+            quantise(step + 1)
+            project(step + 1, 0)
+            project(step + 1, 1)
+            residual(step, 2)
+            mean(step - 1)
+            make_gain(step - LAG)
+            residual(step, 3)
+            variance(step - 1)
+            make_shift(step - LAG)
+            project(step + 1, 2)
+            project(step + 1, 3)
+            squares(step, 0)
+            squares(step, 1)
+            inv_std(step - 1)
+            normalise(step - LAG)

@@ -45,15 +45,14 @@ def tile_crossattention_pa_kernel(tc, feat, h_attn, w_out, b_out, gamma, beta, o
     with ExitStack() as ctx:
         const = ctx.enter_context(tc.tile_pool(name="const", bufs=1))
         raw = ctx.enter_context(tc.tile_pool(name="raw", bufs=SLABS))
-        feats = ctx.enter_context(tc.tile_pool(name="feats", bufs=TOTAL))
         grouped = ctx.enter_context(tc.tile_pool(name="grouped", bufs=2))
+        feats = ctx.enter_context(tc.tile_pool(name="feats", bufs=TOTAL))
         xs = ctx.enter_context(tc.tile_pool(name="xs", bufs=9))
-        scratch = ctx.enter_context(tc.tile_pool(name="scratch", bufs=3))
+        junk = ctx.enter_context(tc.tile_pool(name="junk", bufs=3))
         small = ctx.enter_context(tc.tile_pool(name="small", bufs=LAG + 2))
-        psum_y = ctx.enter_context(tc.psum_pool(name="psum_y", bufs=ROWS))
+        psum_y = ctx.enter_context(tc.psum_pool(name="psum_y", bufs=ROWS + 1))
         psum_t = ctx.enter_context(tc.psum_pool(name="psum_t", bufs=2))
         psum_s = ctx.enter_context(tc.psum_pool(name="psum_s", bufs=1))
-        psum_const = ctx.enter_context(tc.psum_pool(name="psum_const", bufs=1))
 
         eps = const.tile([P, 1], F32)
         nc.vector.memset(eps[:], EPS)
@@ -197,7 +196,7 @@ def tile_crossattention_pa_kernel(tc, feat, h_attn, w_out, b_out, gamma, beta, o
         def squares(i, half):
             if i >= TOTAL:
                 return
-            sq = scratch.tile([P, HALF * N], BF16)
+            sq = junk.tile([P, HALF * N], BF16)
             nc.scalar.activation(
                 out=sq[:],
                 in_=x_sb[i][:, half * HALF : (half + 1) * HALF, :].rearrange("p j n -> p (j n)"),
@@ -250,7 +249,7 @@ def tile_crossattention_pa_kernel(tc, feat, h_attn, w_out, b_out, gamma, beta, o
                 return
             gain = small.tile([P, ROWS], F32)
             nc.vector.tensor_scalar(
-                out=gain[:], in0=gamma_of[:, i % SLABS, :], scalar1=rstd_sb[i][:, 0:1], scalar2=None, op0=ALU.mult
+                out=gain[:], in0=params[:, 1, i % SLABS, :], scalar1=rstd_sb[i][:, 0:1], scalar2=None, op0=ALU.mult
             )
             gain_sb[i] = gain
 
@@ -262,7 +261,7 @@ def tile_crossattention_pa_kernel(tc, feat, h_attn, w_out, b_out, gamma, beta, o
                 out=shift[:],
                 in0=gain_sb[i][:],
                 scalar=neg_mean_sb[i][:, 0:1],
-                in1=beta_of[:, i % SLABS, :],
+                in1=params[:, 2, i % SLABS, :],
                 op0=ALU.mult,
                 op1=ALU.add,
             )
@@ -300,32 +299,22 @@ def tile_crossattention_pa_kernel(tc, feat, h_attn, w_out, b_out, gamma, beta, o
         nc.vector.tensor_copy(out=params[:], in_=params_bf[:])
         for j in range(ROWS):
             project(0, j)
-        affine_ps = psum_const.tile([P, 2, SLABS, ROWS], F32)
-        nc.tensor.matmul(
-            out=affine_ps[:].rearrange("p a s j -> p (a s j)"),
-            lhsT=ident[:],
-            rhs=params[:, 1:3].rearrange("p a s j -> p (a s j)"),
-            start=True,
-            stop=True,
-        )
-        gamma_of = affine_ps[:, 0]
-        beta_of = affine_ps[:, 1]
 
         for step in range(TOTAL + LAG):
+            quantise(step + 1)
             regroup(step + 2)
             residual(step, 0)
-            residual(step, 1)
-            quantise(step + 1)
             project(step + 1, 0)
+            residual(step, 1)
             project(step + 1, 1)
             residual(step, 2)
+            project(step + 1, 2)
             mean(step - 1)
             make_gain(step - LAG)
             residual(step, 3)
+            project(step + 1, 3)
             variance(step - 1)
             make_shift(step - LAG)
-            project(step + 1, 2)
-            project(step + 1, 3)
             squares(step, 0)
             squares(step, 1)
             inv_std(step - 1)

from contextlib import ExitStack

import concourse.mybir as mybir
from concourse.masks import make_identity

F32 = mybir.dt.float32
BF16 = mybir.dt.bfloat16
U32 = mybir.dt.uint32
U8 = mybir.dt.uint8
FP8X4 = mybir.dt.float8_e4m3fn_x4
ALU = mybir.AluOpType
ACT = mybir.ActivationFunctionType
AX = mybir.AxisListType

P = 128
PACK = 4
BATCH = 4
CHANNELS = 2048
K = P * PACK
N = 512
GROUP = 128
EPS = 1e-5

ROWS = 4
HALF = ROWS // 2
SLAB = P * ROWS
SLABS = CHANNELS // SLAB
TOTAL = BATCH * SLABS
QUADRANT = GROUP // ROWS
LAG = 2
ROWS_ON_SCALAR = 1
BLOCK = 8

FLOPS = 2 * BATCH * CHANNELS * K * N


def tile_crossattention_pa_kernel(tc, feat, h_attn, w_out, b_out, gamma, beta, out):
    nc = tc.nc

    feat_v = feat.rearrange("b (s p j) h w -> (b s) p j (h w)", p=P, j=ROWS)
    out_v = out.rearrange("b (s p j) h w -> (b s) p j (h w)", p=P, j=ROWS)
    w_v = w_out.rearrange("(s p j) k -> s p j k", p=P, j=ROWS)
    h_v = h_attn.rearrange("b (u q e) h w -> b q u e (h w)", u=2, e=2)

    with ExitStack() as ctx:
        const = ctx.enter_context(tc.tile_pool(name="const", bufs=1))
        raw = ctx.enter_context(tc.tile_pool(name="raw", bufs=SLABS))
        grouped = ctx.enter_context(tc.tile_pool(name="grouped", bufs=2))
        feats = ctx.enter_context(tc.tile_pool(name="feats", bufs=TOTAL))
        xs = ctx.enter_context(tc.tile_pool(name="xs", bufs=9))
        junk = ctx.enter_context(tc.tile_pool(name="junk", bufs=3))
        small = ctx.enter_context(tc.tile_pool(name="small", bufs=LAG + 2))
        psum_y = ctx.enter_context(tc.psum_pool(name="psum_y", bufs=ROWS + 1))
        psum_t = ctx.enter_context(tc.psum_pool(name="psum_t", bufs=2))
        psum_s = ctx.enter_context(tc.psum_pool(name="psum_s", bufs=1))

        eps = const.tile([P, 1], F32)
        nc.vector.memset(eps[:], EPS)
        warm = const.tile([P, 1], F32)
        nc.scalar.activation(out=warm[:], in_=eps[:], func=ACT.Abs_reciprocal_sqrt)

        ident = const.tile([P, P], F32)
        make_identity(nc, ident[:])

        group_avg = const.tile([P, P], F32)
        nc.vector.memset(group_avg[:], 0.0)
        for g in range(P // QUADRANT):
            quadrant = slice(g * QUADRANT, (g + 1) * QUADRANT)
            nc.vector.memset(group_avg[quadrant, quadrant], -1.0 / (GROUP * N))

        params_bf = const.tile([P, 3, SLABS, ROWS], BF16)
        for which, vec in enumerate((b_out, gamma, beta)):
            nc.scalar.dma_start(
                out=params_bf[:, which], in_=vec.rearrange("(s p j) -> p s j", p=P, j=ROWS)
            )
        params = const.tile([P, 3, SLABS, ROWS], F32)

        w_codes = const.tile([P, SLABS, SLAB], U32, align_bytes=64)
        w_scales = const.tile([P, SLABS, SLAB], U8, align_bytes=64)
        h_codes = const.tile([P, BATCH, N], U32, align_bytes=64)
        h_scales = const.tile([P, BATCH, N], U8, align_bytes=64)

        w_raw = {}
        h_raw = {}
        w_grouped = {}
        h_grouped = {}
        feat_sb = {}
        y_ps = {}
        x_sb = {}
        sums_sb = {}
        mom_ps = {}
        neg_mean_sb = {}
        neg_var_sb = {}
        rstd_sb = {}
        gain_sb = {}
        shift_sb = {}

        def new_operands(i):
            b, s = divmod(i, SLABS)
            return i < TOTAL and b == 0, i < TOTAL and s == 0

        def load_operands(i):
            b, s = divmod(i, SLABS)
            new_w, new_h = new_operands(i)
            if new_w:
                w_tile = raw.tile([P, ROWS, K], BF16)
                nc.sync.dma_start(out=w_tile[:], in_=w_v[s])
                w_raw[s] = w_tile
            if new_h:
                h_tile = raw.tile([P, PACK, N], BF16)
                nc.sync.dma_start(out=h_tile[:].rearrange("q (u e) n -> q u e n", u=2), in_=h_v[b])
                h_raw[b] = h_tile

        def load_feat(i):
            feat_tile = feats.tile([P, ROWS, N], BF16)
            nc.sync.dma_start(out=feat_tile[:], in_=feat_v[i])
            feat_sb[i] = feat_tile

        def regroup(i):
            b, s = divmod(i, SLABS)
            new_w, new_h = new_operands(i)
            if new_w:
                w_words = w_raw[s][:].rearrange("p j k -> p (j k)").bitcast(F32)
                w_group = grouped.tile([P, ROWS * P * PACK], BF16, align_bytes=64)
                w_group_words = w_group[:].bitcast(F32).rearrange("q (j p u) -> q j p u", j=ROWS, u=2)
                for half in range(2):
                    w_t = psum_t.tile([P, HALF, 2, P], F32)
                    for r in range(HALF):
                        for u in range(2):
                            first = ((half * HALF + r) * 2 + u) * P
                            nc.tensor.transpose(w_t[:, r, u, :], w_words[:, first : first + P], ident[:])
                    nc.scalar.copy(
                        out=w_group_words[:, half * HALF : (half + 1) * HALF],
                        in_=w_t[:].rearrange("q r u p -> q r p u"),
                    )
                w_grouped[s] = w_group
            if new_h:
                h_group = grouped.tile([P, N, PACK], BF16, align_bytes=64)
                nc.vector.tensor_copy(
                    out=h_group[:].rearrange("q (c i) t -> q c t i", i=4),
                    in_=h_raw[b][:].rearrange("q t (c i) -> q c t i", i=4),
                )
                h_grouped[b] = h_group

        def quantise(i):
            b, s = divmod(i, SLABS)
            new_w, new_h = new_operands(i)
            if new_w:
                nc.vector.quantize_mx(
                    out=w_codes[:, s, :].bitcast(FP8X4), scales=w_scales[:, s, :], in_=w_grouped[s][:]
                )
            if new_h:
                nc.vector.quantize_mx(
                    out=h_codes[:, b, :].bitcast(FP8X4),
                    scales=h_scales[:, b, :],
                    in_=h_grouped[b][:].rearrange("q n t -> q (n t)"),
                )

        def project(i, j):
            if i >= TOTAL:
                return
            b, s = divmod(i, SLABS)
            y = psum_y.tile([P, N], F32)
            cols = slice(j * P, (j + 1) * P)
            nc.tensor.matmul_mx(
                out=y[:],
                lhsT=w_codes[:, s, cols].bitcast(FP8X4),
                lhsT_scale=w_scales[:, s, cols],
                rhs=h_codes[:, b, :].bitcast(FP8X4),
                rhs_scale=h_scales[:, b, :],
                start=True,
                stop=True,
            )
            y_ps[(i, j)] = y

        def residual(i, j):
            if i >= TOTAL:
                return
            s = i % SLABS
            half, r = divmod(j, HALF)
            if j == 0:
                x = xs.tile([P, ROWS, N], F32)
                x_sb[i] = x
                sums = small.tile([P, 2, HALF + 1, BLOCK], F32)
                sums_sb[i] = sums
            nc.vector.scalar_tensor_tensor(
                out=x_sb[i][:, j, :],
                in0=y_ps[(i, j)][:],
                scalar=params[:, 0, s, j : j + 1],
                in1=feat_sb[i][:, j, :],
                op0=ALU.add,
                op1=ALU.add,
                accum_out=sums_sb[i][:, half, r, 0:1],
            )

        def squares(i, half):
            if i >= TOTAL:
                return
            sq = junk.tile([P, HALF * N], BF16)
            nc.scalar.activation(
                out=sq[:],
                in_=x_sb[i][:, half * HALF : (half + 1) * HALF, :].rearrange("p j n -> p (j n)"),
                func=ACT.Square,
                accum_out=sums_sb[i][:, half, HALF, 0:1],
            )
            if half == 0:
                mom = psum_s.tile([P, HALF + 1], F32)
                mom_ps[i] = mom
            nc.tensor.matmul(
                out=mom_ps[i][:],
                lhsT=group_avg[:],
                rhs=sums_sb[i][:, half, :, 0],
                start=(half == 0),
                stop=(half == 1),
            )

        def mean(i):
            if not 0 <= i < TOTAL:
                return
            neg_mean = small.tile([P, 1], F32)
            nc.vector.tensor_reduce(out=neg_mean[:], in_=mom_ps[i][:, 0:HALF], axis=AX.X, op=ALU.add)
            neg_mean_sb[i] = neg_mean

        def variance(i):
            if not 0 <= i < TOTAL:
                return
            neg_var = small.tile([P, 1], F32)
            nc.vector.scalar_tensor_tensor(
                out=neg_var[:],
                in0=neg_mean_sb[i][:],
                scalar=neg_mean_sb[i][:, 0:1],
                in1=mom_ps[i][:, HALF : HALF + 1],
                op0=ALU.mult,
                op1=ALU.add,
            )
            neg_var_sb[i] = neg_var

        def inv_std(i):
            if not 0 <= i < TOTAL:
                return
            rstd = small.tile([P, 1], F32)
            nc.scalar.activation(
                out=rstd[:], in_=neg_var_sb[i][:], func=ACT.Abs_reciprocal_sqrt, bias=eps[:, 0:1], scale=-1.0
            )
            rstd_sb[i] = rstd

        def make_gain(i):
            if not 0 <= i < TOTAL:
                return
            gain = small.tile([P, ROWS], F32)
            nc.vector.tensor_scalar(
                out=gain[:], in0=params[:, 1, i % SLABS, :], scalar1=rstd_sb[i][:, 0:1], scalar2=None, op0=ALU.mult
            )
            gain_sb[i] = gain

        def make_shift(i):
            if not 0 <= i < TOTAL:
                return
            shift = small.tile([P, ROWS], F32)
            nc.vector.scalar_tensor_tensor(
                out=shift[:],
                in0=gain_sb[i][:],
                scalar=neg_mean_sb[i][:, 0:1],
                in1=params[:, 2, i % SLABS, :],
                op0=ALU.mult,
                op1=ALU.add,
            )
            shift_sb[i] = shift

        def normalise(i):
            if not 0 <= i < TOTAL:
                return
            x = x_sb[i]
            helper = nc.vector if i >= TOTAL - LAG else nc.gpsimd
            for j in range(ROWS):
                gain_j = gain_sb[i][:, j : j + 1]
                shift_j = shift_sb[i][:, j : j + 1]
                if j < ROWS_ON_SCALAR:
                    nc.scalar.activation(out=x[:, j, :], in_=x[:, j, :], func=ACT.Identity, bias=shift_j, scale=gain_j)
                else:
                    helper.tensor_scalar(
                        out=x[:, j, :], in0=x[:, j, :], scalar1=gain_j, scalar2=shift_j, op0=ALU.mult, op1=ALU.add
                    )
            for half in range(2):
                rows = slice(half * HALF, (half + 1) * HALF)
                nc.sync.dma_start(out=out_v[i][:, rows, :], in_=x[:, rows, :])

        ctx.enter_context(tc.manual_schedule())

        load_operands(0)
        load_operands(1)
        for i in range(TOTAL):
            load_feat(i)
            load_operands(i + 2)

        regroup(0)
        regroup(1)
        quantise(0)
        nc.vector.tensor_copy(out=params[:], in_=params_bf[:])
        for j in range(ROWS):
            project(0, j)

        for step in range(TOTAL + LAG):
            quantise(step + 1)
            regroup(step + 2)
            residual(step, 0)
            project(step + 1, 0)
            residual(step, 1)
            project(step + 1, 1)
            residual(step, 2)
            project(step + 1, 2)
            mean(step - 1)
            make_gain(step - LAG)
            residual(step, 3)
            project(step + 1, 3)
            variance(step - 1)
            make_shift(step - LAG)
            squares(step, 0)
            squares(step, 1)
            inv_std(step - 1)
            normalise(step - LAG)
